import numpy as np
import ml_dtypes


def mxq(x, axis, fmt="e4m3"):
    dtype, down = {"e4m3": (ml_dtypes.float8_e4m3fn, 7), "e5m2": (ml_dtypes.float8_e5m2, 14)}[fmt]
    v = np.moveaxis(np.asarray(x, np.float32).astype(ml_dtypes.bfloat16).astype(np.float64), axis, -1)
    blocks = v.reshape(v.shape[:-1] + (-1, 32))
    amax = np.abs(blocks).max(-1, keepdims=True)
    byte = np.maximum(np.where(amax > 0, np.frexp(amax)[1] - 1 + 127, 0) - down, 1)
    scale = np.exp2(byte - 127.0)
    codes = (blocks / scale).astype(np.float32).astype(dtype).astype(np.float64)
    return np.moveaxis((codes * scale).reshape(v.shape), -1, axis)


WIDE = False


def mx_kscale(k):
    if not WIDE:
        return np.ones(k)
    levels = np.array([20, -20, 10, -10, 0])
    a = np.random.permutation(np.resize(levels, k // 512 * 4)).reshape(k // 512, 4)
    idx = np.arange(k)
    return np.exp2(a[idx // 512, idx % 128 // 32])


BF16 = ml_dtypes.bfloat16


def bf(x):
    return np.asarray(x, np.float32).astype(BF16)


def f64(x):
    return np.asarray(x).astype(np.float64)


B, S, D, H = 2, 512, 1024, 8
DH = D // H


def softmax(v, axis):
    e = np.exp(v - v.max(axis, keepdims=True))
    return e / e.sum(axis, keepdims=True)


def setup_inputs():
    u = mx_kscale(D)
    q_soft = softmax(np.random.standard_normal((B, H, S, DH)) * 1.5, -1)
    kv = np.random.standard_normal((B, H, DH, DH)) * 6.0 * np.sqrt(S) / DH
    W_O = np.random.standard_normal((D, H * DH)) * 2.0 / np.sqrt(D) / u[:, None]
    g = np.random.standard_normal((B, S, D)) * np.exp2(np.random.randint(-12, 1, (B, S, 1))) * u
    return {"q_soft": bf(q_soft), "kv": bf(kv), "W_O": bf(W_O), "grad_out": bf(g)}


def reference(q_soft, kv, W_O, grad_out):
    gy = mxq(f64(grad_out), 2, "e5m2") @ mxq(f64(W_O), 0, "e4m3")
    gbt = gy.reshape(B, H, S, DH)
    return gbt @ f64(kv).transpose(0, 1, 3, 2)

@@ -1,0 +1,184 @@
+from contextlib import ExitStack
+
+import concourse.masks as masks
+import concourse.mybir as mybir
+
+F32 = mybir.dt.float32
+BF16 = mybir.dt.bfloat16
+U32 = mybir.dt.uint32
+U8 = mybir.dt.uint8
+E4M3_X4 = mybir.dt.float8_e4m3fn_x4
+E5M2_X4 = mybir.dt.float8_e5m2_x4
+
+P = 128
+B, S, D, H = 2, 512, 1024, 8
+DH = D // H
+PACK = 4
+K_PASS = P * PACK
+PASSES = D // K_PASS
+TOKEN_BLOCKS = S // P
+HEAD_ROWS = S // H
+CHUNKS = D // DH
+HALF = CHUNKS // 2
+HALF_COLS = HALF * DH
+QUARTER_COLS = HALF_COLS // 2
+
+FLOPS = 2 * B * S * D * D + 2 * B * H * S * DH * DH
+BYTES = 2 * (B * H * DH * DH + D * D + B * S * D) + 4 * B * H * S * DH
+
+
+def tile_mhla2_pb_kernel(tc, q_soft, kv, W_O, grad_out, out):
+    nc = tc.nc
+    with ExitStack() as ctx:
+        keep = ctx.enter_context(tc.tile_pool(name="keep", bufs=1))
+        stage = ctx.enter_context(tc.tile_pool(name="stage", bufs=4))
+        banks = ctx.enter_context(tc.psum_pool(name="banks", bufs=8))
+
+        ident_f32 = keep.tile([P, P], F32)
+        masks.make_identity(nc, ident_f32[:])
+        ident_bf16 = keep.tile([P, P], BF16)
+        masks.make_identity(nc, ident_bf16[:])
+
+        tokens_raw = [
+            [keep.tile([P, D], BF16, name="tokens_raw_%d_%d" % (b, tb)) for tb in range(TOKEN_BLOCKS)]
+            for b in range(B)
+        ]
+        tokens_grouped = [
+            keep.tile([P, PASSES * S * PACK], BF16, name="tokens_grouped_%d" % b, align_bytes=64) for b in range(B)
+        ]
+        tokens_codes = [keep.tile([P, PASSES, S], U32, name="tokens_codes_%d" % b, align_bytes=64) for b in range(B)]
+        tokens_scales = [keep.tile([P, PASSES, S], U8, name="tokens_scales_%d" % b, align_bytes=64) for b in range(B)]
+        w_raw = keep.tile([P, PASSES, PACK, D], BF16)
+        w_grouped = keep.tile([P, PASSES, D, PACK], BF16, align_bytes=64)
+        w_codes = keep.tile([P, PASSES, D], U32, align_bytes=64)
+        w_scales = keep.tile([P, PASSES, D], U8, align_bytes=64)
+        kv_raw = [keep.tile([P, H, DH], BF16, name="kv_raw_%d" % b) for b in range(B)]
+        kv_t = [keep.tile([P, H, DH], F32, name="kv_t_%d" % b) for b in range(B)]
+        gy_t = [keep.tile([P, H, HALF, P], F32, name="gy_t_%d" % b) for b in range(B)]
+
+        def copy_out_of_psum(index, dst, src):
+            if index % 2 == 0:
+                nc.vector.tensor_copy(out=dst, in_=src)
+            else:
+                nc.scalar.copy(out=dst, in_=src)
+
+        def load_tokens(b):
+            for tb in range(TOKEN_BLOCKS):
+                nc.sync.dma_start(out=tokens_raw[b][tb][:], in_=grad_out[b, P * tb : P * (tb + 1), :])
+
+        def load_weights(half):
+            cols = slice(HALF_COLS * half, HALF_COLS * (half + 1))
+            for g in range(PASSES):
+                for u in range(2):
+                    first = K_PASS * g + 2 * P * u
+                    nc.sync.dma_start(
+                        out=w_raw[:, g, 2 * u : 2 * u + 2, cols],
+                        in_=W_O[first : first + 2 * P, cols].rearrange("(p e) i -> p e i", e=2),
+                    )
+
+        def load_kv(b):
+            nc.sync.dma_start(out=kv_raw[b][:], in_=kv[b].rearrange("h d e -> d h e"))
+
+        def quantise_tokens(b):
+            grouped_words = tokens_grouped[b][:].bitcast(F32).rearrange("p (g r u) -> p g r u", g=PASSES, u=2)
+            for tb in range(TOKEN_BLOCKS):
+                words = tokens_raw[b][tb][:].bitcast(F32)
+                words_t = banks.tile([P, PASSES, 2, P], F32, tag="bank")
+                for g in range(PASSES):
+                    for u in range(2):
+                        first = (2 * g + u) * P
+                        nc.tensor.transpose(words_t[:, g, u, :], words[:, first : first + P], ident_f32[:])
+                copy_out_of_psum(
+                    tb,
+                    grouped_words[:, :, P * tb : P * (tb + 1), :],
+                    words_t[:].rearrange("p g u r -> p g r u"),
+                )
+            for g in range(PASSES):
+                nc.vector.quantize_mx(
+                    out=tokens_codes[b][:, g, :].bitcast(E5M2_X4),
+                    scales=tokens_scales[b][:, g, :],
+                    in_=tokens_grouped[b][:, S * PACK * g : S * PACK * (g + 1)],
+                )
+
+        def quantise_weights(half):
+            for g in range(PASSES):
+                for quarter in range(2):
+                    first = HALF_COLS * half + QUARTER_COLS * quarter
+                    cols = slice(first, first + QUARTER_COLS)
+                    dst = w_grouped[:, g, cols, :].rearrange("p (c i) t -> p c t i", i=4)
+                    src = w_raw[:, g, :, cols].rearrange("p t (c i) -> p c t i", i=4)
+                    if quarter == 0:
+                        nc.vector.tensor_copy(out=dst, in_=src)
+                    else:
+                        nc.scalar.copy(out=dst, in_=src)
+                for quarter in range(2):
+                    first = HALF_COLS * half + QUARTER_COLS * quarter
+                    cols = slice(first, first + QUARTER_COLS)
+                    nc.vector.quantize_mx(
+                        out=w_codes[:, g, cols].bitcast(E4M3_X4),
+                        scales=w_scales[:, g, cols],
+                        in_=w_grouped[:, g, cols, :].rearrange("p i t -> p (i t)"),
+                    )
+
+        def transpose_kv(b):
+            kv_bank = banks.tile([P, H, DH], BF16, tag="bank")
+            for h in range(H):
+                nc.tensor.transpose(kv_bank[:, h, :], kv_raw[b][:, h, :], ident_bf16[:])
+            for part in range(2):
+                heads = slice(HALF * part, HALF * (part + 1))
+                copy_out_of_psum(part, kv_t[b][:, heads, :], kv_bank[:, heads, :])
+
+        def project(b, half):
+            accs = [banks.tile([P, S], F32, tag="bank", name="gy_bank_%d" % j) for j in range(HALF)]
+            for g in range(PASSES):
+                for j in range(HALF):
+                    cols = slice(DH * (HALF * half + j), DH * (HALF * half + j + 1))
+                    nc.tensor.matmul_mx(
+                        out=accs[j][:],
+                        lhsT=w_codes[:, g, cols].bitcast(E4M3_X4),
+                        lhsT_scale=w_scales[:, g, cols],
+                        rhs=tokens_codes[b][:, g, :].bitcast(E5M2_X4),
+                        rhs_scale=tokens_scales[b][:, g, :],
+                        start=(g == 0),
+                        stop=(g == PASSES - 1),
+                    )
+            for j in range(HALF):
+                copy_out_of_psum(
+                    j,
+                    gy_t[b][:, :, j, HEAD_ROWS * half : HEAD_ROWS * (half + 1)],
+                    accs[j][:].rearrange("p (h r) -> p h r", h=H),
+                )
+
+        def read_out(b, heads):
+            for h in heads:
+                out_bank = banks.tile([P, HALF, DH], F32, tag="bank")
+                for j in range(HALF):
+                    nc.tensor.matmul(
+                        out=out_bank[:, j, :], lhsT=gy_t[b][:, h, j, :], rhs=kv_t[b][:, h, :], start=True, stop=True
+                    )
+                out_rows = stage.tile([P, HALF * DH], F32)
+                copy_out_of_psum(h, out_rows[:], out_bank[:].rearrange("p j d -> p (j d)"))
+                dst = out[b, h].rearrange("(r cc j) d -> cc r (j d)", cc=2, j=HALF)
+                for cc in range(2):
+                    nc.sync.dma_start(out=dst[cc], in_=out_rows[HEAD_ROWS * cc : HEAD_ROWS * (cc + 1), :])
+
+        load_tokens(0)
+        load_weights(0)
+        load_kv(0)
+        load_weights(1)
+        load_tokens(1)
+        load_kv(1)
+
+        quantise_tokens(0)
+        quantise_weights(0)
+        project(0, 0)
+        transpose_kv(0)
+        quantise_weights(1)
+        project(0, 1)
+        quantise_tokens(1)
+        transpose_kv(1)
+        read_out(0, range(0, HALF))
+        project(1, 0)
+        project(1, 1)
+        read_out(0, range(HALF, H))
+        read_out(1, range(0, H))

@@ -33,6 +33,7 @@ def tile_mhla2_pb_kernel(tc, q_soft, kv, W_O, grad_out, out):
         keep = ctx.enter_context(tc.tile_pool(name="keep", bufs=1))
         stage = ctx.enter_context(tc.tile_pool(name="stage", bufs=4))
         banks = ctx.enter_context(tc.psum_pool(name="banks", bufs=8))
+        ctx.enter_context(tc.manual_schedule())
 
         ident_f32 = keep.tile([P, P], F32)
         masks.make_identity(nc, ident_f32[:])
@@ -54,7 +55,7 @@ def tile_mhla2_pb_kernel(tc, q_soft, kv, W_O, grad_out, out):
         w_scales = keep.tile([P, PASSES, D], U8, align_bytes=64)
         kv_raw = [keep.tile([P, H, DH], BF16, name="kv_raw_%d" % b) for b in range(B)]
         kv_t = [keep.tile([P, H, DH], F32, name="kv_t_%d" % b) for b in range(B)]
-        gy_t = [keep.tile([P, H, HALF, P], F32, name="gy_t_%d" % b) for b in range(B)]
+        gy_t = [[keep.tile([P, H, P], F32, name="gy_t_%d_%d" % (b, j)) for j in range(HALF)] for b in range(B)]
 
         def copy_out_of_psum(index, dst, src):
             if index % 2 == 0:
@@ -100,20 +101,23 @@ def tile_mhla2_pb_kernel(tc, q_soft, kv, W_O, grad_out, out):
                     in_=tokens_grouped[b][:, S * PACK * g : S * PACK * (g + 1)],
                 )
 
+        def quarter_cols(half, quarter):
+            first = HALF_COLS * half + QUARTER_COLS * quarter
+            return slice(first, first + QUARTER_COLS)
+
         def quantise_weights(half):
             for g in range(PASSES):
                 for quarter in range(2):
-                    first = HALF_COLS * half + QUARTER_COLS * quarter
-                    cols = slice(first, first + QUARTER_COLS)
+                    cols = quarter_cols(half, quarter)
                     dst = w_grouped[:, g, cols, :].rearrange("p (c i) t -> p c t i", i=4)
                     src = w_raw[:, g, :, cols].rearrange("p t (c i) -> p c t i", i=4)
                     if quarter == 0:
                         nc.vector.tensor_copy(out=dst, in_=src)
                     else:
                         nc.scalar.copy(out=dst, in_=src)
+            for g in range(PASSES):
                 for quarter in range(2):
-                    first = HALF_COLS * half + QUARTER_COLS * quarter
-                    cols = slice(first, first + QUARTER_COLS)
+                    cols = quarter_cols(half, quarter)
                     nc.vector.quantize_mx(
                         out=w_codes[:, g, cols].bitcast(E4M3_X4),
                         scales=w_scales[:, g, cols],
@@ -124,17 +128,16 @@ def tile_mhla2_pb_kernel(tc, q_soft, kv, W_O, grad_out, out):
             kv_bank = banks.tile([P, H, DH], BF16, tag="bank")
             for h in range(H):
                 nc.tensor.transpose(kv_bank[:, h, :], kv_raw[b][:, h, :], ident_bf16[:])
-            for part in range(2):
-                heads = slice(HALF * part, HALF * (part + 1))
-                copy_out_of_psum(part, kv_t[b][:, heads, :], kv_bank[:, heads, :])
+            for heads in (slice(0, H // 2), slice(H // 2, H)):
+                nc.vector.tensor_copy(out=kv_t[b][:, heads, :], in_=kv_bank[:, heads, :])
 
         def project(b, half):
-            accs = [banks.tile([P, S], F32, tag="bank", name="gy_bank_%d" % j) for j in range(HALF)]
+            gy_banks = [banks.tile([P, S], F32, tag="bank", name="gy_bank_%d" % j) for j in range(HALF)]
             for g in range(PASSES):
                 for j in range(HALF):
                     cols = slice(DH * (HALF * half + j), DH * (HALF * half + j + 1))
                     nc.tensor.matmul_mx(
-                        out=accs[j][:],
+                        out=gy_banks[j][:],
                         lhsT=w_codes[:, g, cols].bitcast(E4M3_X4),
                         lhsT_scale=w_scales[:, g, cols],
                         rhs=tokens_codes[b][:, g, :].bitcast(E5M2_X4),
@@ -142,11 +145,14 @@ def tile_mhla2_pb_kernel(tc, q_soft, kv, W_O, grad_out, out):
                         start=(g == 0),
                         stop=(g == PASSES - 1),
                     )
+            return gy_banks
+
+        def keep_projection(b, half, gy_banks):
             for j in range(HALF):
                 copy_out_of_psum(
-                    j,
-                    gy_t[b][:, :, j, HEAD_ROWS * half : HEAD_ROWS * (half + 1)],
-                    accs[j][:].rearrange("p (h r) -> p h r", h=H),
+                    1 if half == 0 else j + 1,
+                    gy_t[b][j][:, :, HEAD_ROWS * half : HEAD_ROWS * (half + 1)],
+                    gy_banks[j][:].rearrange("p (h r) -> p h r", h=H),
                 )
 
         def read_out(b, heads):
@@ -154,7 +160,7 @@ def tile_mhla2_pb_kernel(tc, q_soft, kv, W_O, grad_out, out):
                 out_bank = banks.tile([P, HALF, DH], F32, tag="bank")
                 for j in range(HALF):
                     nc.tensor.matmul(
-                        out=out_bank[:, j, :], lhsT=gy_t[b][:, h, j, :], rhs=kv_t[b][:, h, :], start=True, stop=True
+                        out=out_bank[:, j, :], lhsT=gy_t[b][j][:, h, :], rhs=kv_t[b][:, h, :], start=True, stop=True
                     )
                 out_rows = stage.tile([P, HALF * DH], F32)
                 copy_out_of_psum(h, out_rows[:], out_bank[:].rearrange("p j d -> p (j d)"))
@@ -164,21 +170,23 @@ def tile_mhla2_pb_kernel(tc, q_soft, kv, W_O, grad_out, out):
 
         load_tokens(0)
         load_weights(0)
-        load_kv(0)
         load_weights(1)
+        load_kv(0)
         load_tokens(1)
         load_kv(1)
 
         quantise_tokens(0)
         quantise_weights(0)
-        project(0, 0)
-        transpose_kv(0)
+        gy_banks = project(0, 0)
         quantise_weights(1)
-        project(0, 1)
+        keep_projection(0, 0, gy_banks)
+        transpose_kv(0)
+        keep_projection(0, 1, project(0, 1))
+
+        read_out(0, range(0, H // 2))
         quantise_tokens(1)
         transpose_kv(1)
-        read_out(0, range(0, HALF))
-        project(1, 0)
-        project(1, 1)
-        read_out(0, range(HALF, H))
+        read_out(0, range(H // 2, H))
+        keep_projection(1, 0, project(1, 0))
+        keep_projection(1, 1, project(1, 1))
         read_out(1, range(0, H))

@@ -165,8 +165,8 @@ def tile_mhla2_pb_kernel(tc, q_soft, kv, W_O, grad_out, out):
                 out_rows = stage.tile([P, HALF * DH], F32)
                 copy_out_of_psum(h, out_rows[:], out_bank[:].rearrange("p j d -> p (j d)"))
                 dst = out[b, h].rearrange("(r cc j) d -> cc r (j d)", cc=2, j=HALF)
-                for cc in range(2):
-                    nc.sync.dma_start(out=dst[cc], in_=out_rows[HEAD_ROWS * cc : HEAD_ROWS * (cc + 1), :])
+                nc.sync.dma_start(out=dst[0], in_=out_rows[:HEAD_ROWS, :])
+                nc.scalar.dma_start(out=dst[1], in_=out_rows[HEAD_ROWS:, :])
 
         load_tokens(0)
         load_weights(0)

@@ -18,9 +18,9 @@ K_PASS = P * PACK
 PASSES = D // K_PASS
 TOKEN_BLOCKS = S // P
 HEAD_ROWS = S // H
-CHUNKS = D // DH
-HALF = CHUNKS // 2
-HALF_COLS = HALF * DH
+HALVES = 2
+HALF_COLS = D // HALVES
+HALF_CHUNKS = HALF_COLS // DH
 QUARTER_COLS = HALF_COLS // 2
 
 FLOPS = 2 * B * S * D * D + 2 * B * H * S * DH * DH
@@ -39,23 +39,31 @@ def tile_mhla2_pb_kernel(tc, q_soft, kv, W_O, grad_out, out):
         masks.make_identity(nc, ident_f32[:])
         ident_bf16 = keep.tile([P, P], BF16)
         masks.make_identity(nc, ident_bf16[:])
+        table_warmer = keep.tile([P, 1], BF16)
+        nc.scalar.copy(out=table_warmer[:], in_=ident_bf16[:, 0:1])
 
         tokens_raw = [
             [keep.tile([P, D], BF16, name="tokens_raw_%d_%d" % (b, tb)) for tb in range(TOKEN_BLOCKS)]
             for b in range(B)
         ]
         tokens_grouped = [
-            keep.tile([P, PASSES * S * PACK], BF16, name="tokens_grouped_%d" % b, align_bytes=64) for b in range(B)
+            keep.tile([P, PASSES, S * PACK], BF16, name="tokens_grouped_%d" % b, align_bytes=64) for b in range(B)
         ]
         tokens_codes = [keep.tile([P, PASSES, S], U32, name="tokens_codes_%d" % b, align_bytes=64) for b in range(B)]
         tokens_scales = [keep.tile([P, PASSES, S], U8, name="tokens_scales_%d" % b, align_bytes=64) for b in range(B)]
-        w_raw = keep.tile([P, PASSES, PACK, D], BF16)
+        w_raw = [
+            [keep.tile([P, PACK, HALF_COLS], BF16, name="w_raw_%d_%d" % (half, g)) for g in range(PASSES)]
+            for half in range(HALVES)
+        ]
         w_grouped = keep.tile([P, PASSES, D, PACK], BF16, align_bytes=64)
         w_codes = keep.tile([P, PASSES, D], U32, align_bytes=64)
         w_scales = keep.tile([P, PASSES, D], U8, align_bytes=64)
         kv_raw = [keep.tile([P, H, DH], BF16, name="kv_raw_%d" % b) for b in range(B)]
         kv_t = [keep.tile([P, H, DH], F32, name="kv_t_%d" % b) for b in range(B)]
-        gy_t = [[keep.tile([P, H, P], F32, name="gy_t_%d_%d" % (b, j)) for j in range(HALF)] for b in range(B)]
+        gy_t = [
+            [[keep.tile([P, H, P], F32, name="gy_t_%d_%d_%d" % (b, half, j)) for j in range(2)] for half in range(HALVES)]
+            for b in range(B)
+        ]
 
         def copy_out_of_psum(index, dst, src):
             if index % 2 == 0:
@@ -67,21 +75,21 @@ def tile_mhla2_pb_kernel(tc, q_soft, kv, W_O, grad_out, out):
             for tb in range(TOKEN_BLOCKS):
                 nc.sync.dma_start(out=tokens_raw[b][tb][:], in_=grad_out[b, P * tb : P * (tb + 1), :])
 
-        def load_weights(half):
+        def load_weights(half, g):
             cols = slice(HALF_COLS * half, HALF_COLS * (half + 1))
-            for g in range(PASSES):
-                for u in range(2):
-                    first = K_PASS * g + 2 * P * u
-                    nc.sync.dma_start(
-                        out=w_raw[:, g, 2 * u : 2 * u + 2, cols],
-                        in_=W_O[first : first + 2 * P, cols].rearrange("(p e) i -> p e i", e=2),
-                    )
+            for u in range(2):
+                first = K_PASS * g + 2 * P * u
+                nc.sync.dma_start(
+                    out=w_raw[half][g][:, 2 * u : 2 * u + 2, :],
+                    in_=W_O[first : first + 2 * P, cols].rearrange("(p e) i -> p e i", e=2),
+                )
 
         def load_kv(b):
             nc.sync.dma_start(out=kv_raw[b][:], in_=kv[b].rearrange("h d e -> d h e"))
 
-        def quantise_tokens(b):
-            grouped_words = tokens_grouped[b][:].bitcast(F32).rearrange("p (g r u) -> p g r u", g=PASSES, u=2)
+        def transpose_tokens(b):
+            grouped_words = tokens_grouped[b][:].rearrange("p g x -> p (g x)").bitcast(F32)
+            grouped_words = grouped_words.rearrange("p (g r u) -> p g r u", g=PASSES, u=2)
             for tb in range(TOKEN_BLOCKS):
                 words = tokens_raw[b][tb][:].bitcast(F32)
                 words_t = banks.tile([P, PASSES, 2, P], F32, tag="bank")
@@ -89,104 +97,117 @@ def tile_mhla2_pb_kernel(tc, q_soft, kv, W_O, grad_out, out):
                     for u in range(2):
                         first = (2 * g + u) * P
                         nc.tensor.transpose(words_t[:, g, u, :], words[:, first : first + P], ident_f32[:])
-                copy_out_of_psum(
-                    tb,
-                    grouped_words[:, :, P * tb : P * (tb + 1), :],
-                    words_t[:].rearrange("p g u r -> p g r u"),
-                )
-            for g in range(PASSES):
-                nc.vector.quantize_mx(
-                    out=tokens_codes[b][:, g, :].bitcast(E5M2_X4),
-                    scales=tokens_scales[b][:, g, :],
-                    in_=tokens_grouped[b][:, S * PACK * g : S * PACK * (g + 1)],
+                nc.scalar.copy(
+                    out=grouped_words[:, :, P * tb : P * (tb + 1), :], in_=words_t[:].rearrange("p g u r -> p g r u")
                 )
 
-        def quarter_cols(half, quarter):
-            first = HALF_COLS * half + QUARTER_COLS * quarter
+        def quantise_tokens(b, g):
+            nc.vector.quantize_mx(
+                out=tokens_codes[b][:, g, :].bitcast(E5M2_X4),
+                scales=tokens_scales[b][:, g, :],
+                in_=tokens_grouped[b][:, g, :],
+            )
+
+        def quarter(half, cc):
+            first = HALF_COLS * half + QUARTER_COLS * cc
             return slice(first, first + QUARTER_COLS)
 
-        def quantise_weights(half):
-            for g in range(PASSES):
-                for quarter in range(2):
-                    cols = quarter_cols(half, quarter)
-                    dst = w_grouped[:, g, cols, :].rearrange("p (c i) t -> p c t i", i=4)
-                    src = w_raw[:, g, :, cols].rearrange("p t (c i) -> p c t i", i=4)
-                    if quarter == 0:
-                        nc.vector.tensor_copy(out=dst, in_=src)
-                    else:
-                        nc.scalar.copy(out=dst, in_=src)
-            for g in range(PASSES):
-                for quarter in range(2):
-                    cols = quarter_cols(half, quarter)
-                    nc.vector.quantize_mx(
-                        out=w_codes[:, g, cols].bitcast(E4M3_X4),
-                        scales=w_scales[:, g, cols],
-                        in_=w_grouped[:, g, cols, :].rearrange("p i t -> p (i t)"),
-                    )
+        def regroup_weights(half, g):
+            for cc in range(2):
+                dst = w_grouped[:, g, quarter(half, cc), :].rearrange("p (c i) t -> p c t i", i=4)
+                src = w_raw[half][g][:, :, QUARTER_COLS * cc : QUARTER_COLS * (cc + 1)].rearrange("p t (c i) -> p c t i", i=4)
+                if cc == 0:
+                    nc.vector.tensor_copy(out=dst, in_=src)
+                else:
+                    nc.scalar.copy(out=dst, in_=src)
+
+        def quantise_weights(half, g):
+            for cc in range(2):
+                nc.vector.quantize_mx(
+                    out=w_codes[:, g, quarter(half, cc)].bitcast(E4M3_X4),
+                    scales=w_scales[:, g, quarter(half, cc)],
+                    in_=w_grouped[:, g, quarter(half, cc), :].rearrange("p i t -> p (i t)"),
+                )
 
         def transpose_kv(b):
             kv_bank = banks.tile([P, H, DH], BF16, tag="bank")
             for h in range(H):
                 nc.tensor.transpose(kv_bank[:, h, :], kv_raw[b][:, h, :], ident_bf16[:])
             for heads in (slice(0, H // 2), slice(H // 2, H)):
-                nc.vector.tensor_copy(out=kv_t[b][:, heads, :], in_=kv_bank[:, heads, :])
+                nc.scalar.copy(out=kv_t[b][:, heads, :], in_=kv_bank[:, heads, :])
 
         def project(b, half):
-            gy_banks = [banks.tile([P, S], F32, tag="bank", name="gy_bank_%d" % j) for j in range(HALF)]
+            gy_banks = [banks.tile([P, S], F32, tag="bank", name="gy_bank_%d" % q) for q in range(HALF_CHUNKS)]
             for g in range(PASSES):
-                for j in range(HALF):
-                    cols = slice(DH * (HALF * half + j), DH * (HALF * half + j + 1))
+                for q in range(HALF_CHUNKS):
+                    first = HALF_COLS * half + DH * q
                     nc.tensor.matmul_mx(
-                        out=gy_banks[j][:],
-                        lhsT=w_codes[:, g, cols].bitcast(E4M3_X4),
-                        lhsT_scale=w_scales[:, g, cols],
+                        out=gy_banks[q][:],
+                        lhsT=w_codes[:, g, first : first + DH].bitcast(E4M3_X4),
+                        lhsT_scale=w_scales[:, g, first : first + DH],
                         rhs=tokens_codes[b][:, g, :].bitcast(E5M2_X4),
                         rhs_scale=tokens_scales[b][:, g, :],
                         start=(g == 0),
                         stop=(g == PASSES - 1),
                     )
-            return gy_banks
-
-        def keep_projection(b, half, gy_banks):
-            for j in range(HALF):
+            for q in range(HALF_CHUNKS):
+                cc, j = divmod(q, 2)
                 copy_out_of_psum(
-                    1 if half == 0 else j + 1,
-                    gy_t[b][j][:, :, HEAD_ROWS * half : HEAD_ROWS * (half + 1)],
-                    gy_banks[j][:].rearrange("p (h r) -> p h r", h=H),
+                    q,
+                    gy_t[b][half][j][:, :, HEAD_ROWS * cc : HEAD_ROWS * (cc + 1)],
+                    gy_banks[q][:].rearrange("p (h r) -> p h r", h=H),
                 )
 
-        def read_out(b, heads):
-            for h in heads:
-                out_bank = banks.tile([P, HALF, DH], F32, tag="bank")
-                for j in range(HALF):
-                    nc.tensor.matmul(
-                        out=out_bank[:, j, :], lhsT=gy_t[b][j][:, h, :], rhs=kv_t[b][:, h, :], start=True, stop=True
-                    )
-                out_rows = stage.tile([P, HALF * DH], F32)
-                copy_out_of_psum(h, out_rows[:], out_bank[:].rearrange("p j d -> p (j d)"))
-                dst = out[b, h].rearrange("(r cc j) d -> cc r (j d)", cc=2, j=HALF)
-                nc.sync.dma_start(out=dst[0], in_=out_rows[:HEAD_ROWS, :])
-                nc.scalar.dma_start(out=dst[1], in_=out_rows[HEAD_ROWS:, :])
+        def read_out(b, half):
+            for first_head in range(0, H, 2):
+                out_bank = banks.tile([P, 2, 2, DH], F32, tag="bank")
+                for i in range(2):
+                    for j in range(2):
+                        nc.tensor.matmul(
+                            out=out_bank[:, i, j, :],
+                            lhsT=gy_t[b][half][j][:, first_head + i, :],
+                            rhs=kv_t[b][:, first_head + i, :],
+                            start=True,
+                            stop=True,
+                        )
+                out_rows = stage.tile([P, 2, 2 * DH], F32)
+                copy_out_of_psum(first_head // 2, out_rows[:], out_bank[:].rearrange("p i j d -> p i (j d)"))
+                dst = out[b, first_head : first_head + 2].rearrange(
+                    "i (r a cc j) d -> a cc r i (j d)", a=HALVES, cc=2, j=2
+                )
+                for cc in range(2):
+                    nc.sync.dma_start(out=dst[half, cc], in_=out_rows[HEAD_ROWS * cc : HEAD_ROWS * (cc + 1), :, :])
 
         load_tokens(0)
-        load_weights(0)
-        load_weights(1)
+        load_weights(0, 0)
         load_kv(0)
+        load_weights(0, 1)
+        load_weights(1, 0)
+        load_weights(1, 1)
         load_tokens(1)
         load_kv(1)
 
-        quantise_tokens(0)
-        quantise_weights(0)
-        gy_banks = project(0, 0)
-        quantise_weights(1)
-        keep_projection(0, 0, gy_banks)
+        transpose_tokens(0)
+        regroup_weights(0, 0)
+        quantise_tokens(0, 0)
+        quantise_weights(0, 0)
         transpose_kv(0)
-        keep_projection(0, 1, project(0, 1))
-
-        read_out(0, range(0, H // 2))
-        quantise_tokens(1)
+        quantise_tokens(0, 1)
+        regroup_weights(0, 1)
+        quantise_weights(0, 1)
+        project(0, 0)
+        for g in range(PASSES):
+            regroup_weights(1, g)
+        for g in range(PASSES):
+            quantise_weights(1, g)
+        read_out(0, 0)
+        project(0, 1)
+        transpose_tokens(1)
+        for g in range(PASSES):
+            quantise_tokens(1, g)
+        read_out(0, 1)
         transpose_kv(1)
-        read_out(0, range(H // 2, H))
-        keep_projection(1, 0, project(1, 0))
-        keep_projection(1, 1, project(1, 1))
-        read_out(1, range(0, H))
+        project(1, 0)
+        project(1, 1)
+        read_out(1, 0)
+        read_out(1, 1)

@@ -31,7 +31,7 @@ def tile_mhla2_pb_kernel(tc, q_soft, kv, W_O, grad_out, out):
     nc = tc.nc
     with ExitStack() as ctx:
         keep = ctx.enter_context(tc.tile_pool(name="keep", bufs=1))
-        stage = ctx.enter_context(tc.tile_pool(name="stage", bufs=4))
+        stage = ctx.enter_context(tc.tile_pool(name="stage", bufs=8))
         banks = ctx.enter_context(tc.psum_pool(name="banks", bufs=8))
         ctx.enter_context(tc.manual_schedule())
 
@@ -47,7 +47,11 @@ def tile_mhla2_pb_kernel(tc, q_soft, kv, W_O, grad_out, out):
             for b in range(B)
         ]
         tokens_grouped = [
-            keep.tile([P, PASSES, S * PACK], BF16, name="tokens_grouped_%d" % b, align_bytes=64) for b in range(B)
+            [
+                keep.tile([P, PASSES, P * PACK], BF16, name="tokens_grouped_%d_%d" % (b, tb), align_bytes=64)
+                for tb in range(TOKEN_BLOCKS)
+            ]
+            for b in range(B)
         ]
         tokens_codes = [keep.tile([P, PASSES, S], U32, name="tokens_codes_%d" % b, align_bytes=64) for b in range(B)]
         tokens_scales = [keep.tile([P, PASSES, S], U8, name="tokens_scales_%d" % b, align_bytes=64) for b in range(B)]
@@ -87,69 +91,72 @@ def tile_mhla2_pb_kernel(tc, q_soft, kv, W_O, grad_out, out):
         def load_kv(b):
             nc.sync.dma_start(out=kv_raw[b][:], in_=kv[b].rearrange("h d e -> d h e"))
 
-        def transpose_tokens(b):
-            grouped_words = tokens_grouped[b][:].rearrange("p g x -> p (g x)").bitcast(F32)
+        def transpose_tokens(b, tb):
+            grouped_words = tokens_grouped[b][tb][:].rearrange("p g x -> p (g x)").bitcast(F32)
             grouped_words = grouped_words.rearrange("p (g r u) -> p g r u", g=PASSES, u=2)
-            for tb in range(TOKEN_BLOCKS):
-                words = tokens_raw[b][tb][:].bitcast(F32)
-                words_t = banks.tile([P, PASSES, 2, P], F32, tag="bank")
-                for g in range(PASSES):
-                    for u in range(2):
-                        first = (2 * g + u) * P
-                        nc.tensor.transpose(words_t[:, g, u, :], words[:, first : first + P], ident_f32[:])
-                nc.scalar.copy(
-                    out=grouped_words[:, :, P * tb : P * (tb + 1), :], in_=words_t[:].rearrange("p g u r -> p g r u")
-                )
+            words = tokens_raw[b][tb][:].bitcast(F32)
+            words_t = banks.tile([P, PASSES, 2, P], F32, tag="bank")
+            for g in range(PASSES):
+                for u in range(2):
+                    first = (2 * g + u) * P
+                    nc.tensor.transpose(words_t[:, g, u, :], words[:, first : first + P], ident_f32[:])
+            nc.scalar.copy(out=grouped_words, in_=words_t[:].rearrange("p g u r -> p g r u"))
 
-        def quantise_tokens(b, g):
-            nc.vector.quantize_mx(
-                out=tokens_codes[b][:, g, :].bitcast(E5M2_X4),
-                scales=tokens_scales[b][:, g, :],
-                in_=tokens_grouped[b][:, g, :],
-            )
+        def quantise_tokens(b, tb):
+            block = slice(P * tb, P * (tb + 1))
+            for g in range(PASSES):
+                nc.vector.quantize_mx(
+                    out=tokens_codes[b][:, g, block].bitcast(E5M2_X4),
+                    scales=tokens_scales[b][:, g, block],
+                    in_=tokens_grouped[b][tb][:, g, :],
+                )
 
         def quarter(half, cc):
             first = HALF_COLS * half + QUARTER_COLS * cc
             return slice(first, first + QUARTER_COLS)
 
-        def regroup_weights(half, g):
-            for cc in range(2):
-                dst = w_grouped[:, g, quarter(half, cc), :].rearrange("p (c i) t -> p c t i", i=4)
-                src = w_raw[half][g][:, :, QUARTER_COLS * cc : QUARTER_COLS * (cc + 1)].rearrange("p t (c i) -> p c t i", i=4)
-                if cc == 0:
-                    nc.vector.tensor_copy(out=dst, in_=src)
-                else:
-                    nc.scalar.copy(out=dst, in_=src)
+        def regroup_weights(half, g, cc, on_vector):
+            dst = w_grouped[:, g, quarter(half, cc), :].rearrange("p (c i) t -> p c t i", i=4)
+            src = w_raw[half][g][:, :, QUARTER_COLS * cc : QUARTER_COLS * (cc + 1)].rearrange("p t (c i) -> p c t i", i=4)
+            if on_vector:
+                nc.vector.tensor_copy(out=dst, in_=src)
+            else:
+                nc.scalar.copy(out=dst, in_=src)
 
-        def quantise_weights(half, g):
-            for cc in range(2):
-                nc.vector.quantize_mx(
-                    out=w_codes[:, g, quarter(half, cc)].bitcast(E4M3_X4),
-                    scales=w_scales[:, g, quarter(half, cc)],
-                    in_=w_grouped[:, g, quarter(half, cc), :].rearrange("p i t -> p (i t)"),
-                )
+        def quantise_weights(half, g, cc):
+            nc.vector.quantize_mx(
+                out=w_codes[:, g, quarter(half, cc)].bitcast(E4M3_X4),
+                scales=w_scales[:, g, quarter(half, cc)],
+                in_=w_grouped[:, g, quarter(half, cc), :].rearrange("p i t -> p (i t)"),
+            )
 
         def transpose_kv(b):
             kv_bank = banks.tile([P, H, DH], BF16, tag="bank")
             for h in range(H):
                 nc.tensor.transpose(kv_bank[:, h, :], kv_raw[b][:, h, :], ident_bf16[:])
-            for heads in (slice(0, H // 2), slice(H // 2, H)):
-                nc.scalar.copy(out=kv_t[b][:, heads, :], in_=kv_bank[:, heads, :])
+            return kv_bank
 
-        def project(b, half):
-            gy_banks = [banks.tile([P, S], F32, tag="bank", name="gy_bank_%d" % q) for q in range(HALF_CHUNKS)]
-            for g in range(PASSES):
-                for q in range(HALF_CHUNKS):
-                    first = HALF_COLS * half + DH * q
-                    nc.tensor.matmul_mx(
-                        out=gy_banks[q][:],
-                        lhsT=w_codes[:, g, first : first + DH].bitcast(E4M3_X4),
-                        lhsT_scale=w_scales[:, g, first : first + DH],
-                        rhs=tokens_codes[b][:, g, :].bitcast(E5M2_X4),
-                        rhs_scale=tokens_scales[b][:, g, :],
-                        start=(g == 0),
-                        stop=(g == PASSES - 1),
-                    )
+        def copy_kv(b, kv_bank, part):
+            heads = slice(H // 2 * part, H // 2 * (part + 1))
+            nc.scalar.copy(out=kv_t[b][:, heads, :], in_=kv_bank[:, heads, :])
+
+        def open_gy_banks():
+            return [banks.tile([P, S], F32, tag="bank", name="gy_bank_%d" % q) for q in range(HALF_CHUNKS)]
+
+        def project_pass(b, half, g, gy_banks):
+            for q in range(HALF_CHUNKS):
+                first = HALF_COLS * half + DH * q
+                nc.tensor.matmul_mx(
+                    out=gy_banks[q][:],
+                    lhsT=w_codes[:, g, first : first + DH].bitcast(E4M3_X4),
+                    lhsT_scale=w_scales[:, g, first : first + DH],
+                    rhs=tokens_codes[b][:, g, :].bitcast(E5M2_X4),
+                    rhs_scale=tokens_scales[b][:, g, :],
+                    start=(g == 0),
+                    stop=(g == PASSES - 1),
+                )
+
+        def copy_gy(b, half, gy_banks):
             for q in range(HALF_CHUNKS):
                 cc, j = divmod(q, 2)
                 copy_out_of_psum(
@@ -158,56 +165,92 @@ def tile_mhla2_pb_kernel(tc, q_soft, kv, W_O, grad_out, out):
                     gy_banks[q][:].rearrange("p (h r) -> p h r", h=H),
                 )
 
-        def read_out(b, half):
-            for first_head in range(0, H, 2):
-                out_bank = banks.tile([P, 2, 2, DH], F32, tag="bank")
-                for i in range(2):
-                    for j in range(2):
-                        nc.tensor.matmul(
-                            out=out_bank[:, i, j, :],
-                            lhsT=gy_t[b][half][j][:, first_head + i, :],
-                            rhs=kv_t[b][:, first_head + i, :],
-                            start=True,
-                            stop=True,
-                        )
-                out_rows = stage.tile([P, 2, 2 * DH], F32)
-                copy_out_of_psum(first_head // 2, out_rows[:], out_bank[:].rearrange("p i j d -> p i (j d)"))
-                dst = out[b, first_head : first_head + 2].rearrange(
-                    "i (r a cc j) d -> a cc r i (j d)", a=HALVES, cc=2, j=2
-                )
-                for cc in range(2):
-                    nc.sync.dma_start(out=dst[half, cc], in_=out_rows[HEAD_ROWS * cc : HEAD_ROWS * (cc + 1), :, :])
+        def project(b, half):
+            gy_banks = open_gy_banks()
+            for g in range(PASSES):
+                project_pass(b, half, g, gy_banks)
+            copy_gy(b, half, gy_banks)
 
-        load_tokens(0)
+        def read_out_matmul(b, half, head, j, dst):
+            nc.tensor.matmul(
+                out=dst, lhsT=gy_t[b][half][j][:, head, :], rhs=kv_t[b][:, head, :], start=True, stop=True
+            )
+
+        def store(index, b, half, first_head, heads, out_bank):
+            out_rows = stage.tile([P, heads, 2 * DH], F32, tag="out_rows")
+            copy_out_of_psum(index, out_rows[:], out_bank[:].rearrange("p i j d -> p i (j d)"))
+            dst = out[b, first_head : first_head + heads].rearrange(
+                "i (r a cc j) d -> a cc r i (j d)", a=HALVES, cc=2, j=2
+            )
+            for cc in range(2):
+                nc.sync.dma_start(out=dst[half, cc], in_=out_rows[HEAD_ROWS * cc : HEAD_ROWS * (cc + 1), :, :])
+
+        def read_out(b, half, first_head):
+            out_banks = [banks.tile([P, 2, 2, DH], F32, tag="bank", name="out_bank_%d" % k) for k in range(2)]
+            for j in range(2):
+                for i in range(4):
+                    read_out_matmul(b, half, first_head + i, j, out_banks[i // 2][:, i % 2, j, :])
+            for k in range(2):
+                store(k, b, half, first_head + 2 * k, 2, out_banks[k])
+
+        def read_out_last(b, half, first_head):
+            for i in range(4):
+                out_bank = banks.tile([P, 1, 2, DH], F32, tag="bank")
+                for j in range(2):
+                    read_out_matmul(b, half, first_head + i, j, out_bank[:, 0, j, :])
+                store(i + 1, b, half, first_head + i, 1, out_bank)
+
         load_weights(0, 0)
+        load_tokens(0)
         load_kv(0)
         load_weights(0, 1)
-        load_weights(1, 0)
-        load_weights(1, 1)
         load_tokens(1)
         load_kv(1)
+        load_weights(1, 0)
+        load_weights(1, 1)
 
-        transpose_tokens(0)
-        regroup_weights(0, 0)
-        quantise_tokens(0, 0)
-        quantise_weights(0, 0)
-        transpose_kv(0)
-        quantise_tokens(0, 1)
-        regroup_weights(0, 1)
-        quantise_weights(0, 1)
-        project(0, 0)
-        for g in range(PASSES):
-            regroup_weights(1, g)
-        for g in range(PASSES):
-            quantise_weights(1, g)
-        read_out(0, 0)
-        project(0, 1)
-        transpose_tokens(1)
-        for g in range(PASSES):
-            quantise_tokens(1, g)
-        read_out(0, 1)
-        transpose_kv(1)
+        for cc in range(2):
+            regroup_weights(0, 0, cc, True)
+        for cc in range(2):
+            quantise_weights(0, 0, cc)
+        for tb in range(TOKEN_BLOCKS):
+            transpose_tokens(0, tb)
+            quantise_tokens(0, tb)
+        kv_bank = transpose_kv(0)
+        copy_kv(0, kv_bank, 0)
+        regroup_weights(0, 1, 0, True)
+        regroup_weights(0, 1, 1, False)
+        copy_kv(0, kv_bank, 1)
+        for cc in range(2):
+            quantise_weights(0, 1, cc)
+        gy_banks = open_gy_banks()
+        project_pass(0, 0, 0, gy_banks)
+        transpose_tokens(1, 0)
+        project_pass(0, 0, 1, gy_banks)
+        copy_gy(0, 0, gy_banks)
+        for tb in range(1, TOKEN_BLOCKS):
+            transpose_tokens(1, tb)
+        for tb in range(TOKEN_BLOCKS):
+            quantise_tokens(1, tb)
+        kv_bank = transpose_kv(1)
+        for part in range(2):
+            copy_kv(1, kv_bank, part)
+        regroup_weights(1, 0, 0, True)
+        regroup_weights(1, 1, 0, True)
+        regroup_weights(1, 0, 1, False)
+        quantise_weights(1, 0, 0)
+        quantise_weights(1, 1, 0)
+        read_out(0, 0, 0)
+        regroup_weights(1, 1, 1, False)
         project(1, 0)
+        quantise_weights(1, 0, 1)
+        quantise_weights(1, 1, 1)
+        read_out(0, 0, 4)
+        read_out(1, 0, 0)
+        project(0, 1)
+        read_out(1, 0, 4)
         project(1, 1)
-        read_out(1, 0)
-        read_out(1, 1)
+        read_out(0, 1, 0)
+        read_out(0, 1, 4)
+        read_out(1, 1, 0)
+        read_out_last(1, 1, 4)

@@ -42,6 +42,14 @@ def tile_mhla2_pb_kernel(tc, q_soft, kv, W_O, grad_out, out):
         table_warmer = keep.tile([P, 1], BF16)
         nc.scalar.copy(out=table_warmer[:], in_=ident_bf16[:, 0:1])
 
+        zeros = keep.tile([P, S], BF16)
+        nc.vector.memset(zeros[:], 0.0)
+        idle_bank = banks.tile([P, S], F32, tag="bank")
+
+        def keep_clock_up(count):
+            for k in range(count):
+                nc.tensor.matmul(out=idle_bank[:], lhsT=zeros[:, 0:P], rhs=zeros[:], start=True, stop=True)
+
         tokens_raw = [
             [keep.tile([P, D], BF16, name="tokens_raw_%d_%d" % (b, tb)) for tb in range(TOKEN_BLOCKS)]
             for b in range(B)
@@ -213,8 +221,10 @@ def tile_mhla2_pb_kernel(tc, q_soft, kv, W_O, grad_out, out):
             regroup_weights(0, 0, cc, True)
         for cc in range(2):
             quantise_weights(0, 0, cc)
+        keep_clock_up(4)
         for tb in range(TOKEN_BLOCKS):
             transpose_tokens(0, tb)
+            keep_clock_up(1)
             quantise_tokens(0, tb)
         kv_bank = transpose_kv(0)
         copy_kv(0, kv_bank, 0)

@@ -97,7 +97,7 @@ def tile_mhla2_pb_kernel(tc, q_soft, kv, W_O, grad_out, out):
                 )
 
         def load_kv(b):
-            nc.sync.dma_start(out=kv_raw[b][:], in_=kv[b].rearrange("h d e -> d h e"))
+            nc.sync.dma_start(out=kv_raw[b][:], in_=kv[b].rearrange("h d e -> (h d) e").rearrange("(p k) e -> p k e", k=H))
 
         def transpose_tokens(b, tb):
             grouped_words = tokens_grouped[b][tb][:].rearrange("p g x -> p (g x)").bitcast(F32)
@@ -140,13 +140,16 @@ def tile_mhla2_pb_kernel(tc, q_soft, kv, W_O, grad_out, out):
 
         def transpose_kv(b):
             kv_bank = banks.tile([P, H, DH], BF16, tag="bank")
-            for h in range(H):
-                nc.tensor.transpose(kv_bank[:, h, :], kv_raw[b][:, h, :], ident_bf16[:])
+            for k in range(H):
+                nc.tensor.transpose(kv_bank[:, k, :], kv_raw[b][:, k, :], ident_bf16[:])
             return kv_bank
 
         def copy_kv(b, kv_bank, part):
             heads = slice(H // 2 * part, H // 2 * (part + 1))
-            nc.scalar.copy(out=kv_t[b][:, heads, :], in_=kv_bank[:, heads, :])
+            nc.scalar.copy(
+                out=kv_t[b][:, heads, :].rearrange("p h (x k) -> p (h x) k", k=H),
+                in_=kv_bank[:, :, P // 2 * part : P // 2 * (part + 1)].rearrange("p k m -> p m k"),
+            )
 
         def open_gy_banks():
             return [banks.tile([P, S], F32, tag="bank", name="gy_bank_%d" % q) for q in range(HALF_CHUNKS)]

@@ -238,22 +238,23 @@ def tile_mhla2_pb_kernel(tc, q_soft, kv, W_O, grad_out, out):
             quantise_weights(0, 1, cc)
         gy_banks = open_gy_banks()
         project_pass(0, 0, 0, gy_banks)
-        transpose_tokens(1, 0)
+        for tb in range(2):
+            transpose_tokens(1, tb)
         project_pass(0, 0, 1, gy_banks)
         copy_gy(0, 0, gy_banks)
-        for tb in range(1, TOKEN_BLOCKS):
+        for tb in range(2, TOKEN_BLOCKS):
             transpose_tokens(1, tb)
         for tb in range(TOKEN_BLOCKS):
             quantise_tokens(1, tb)
-        kv_bank = transpose_kv(1)
-        for part in range(2):
-            copy_kv(1, kv_bank, part)
         regroup_weights(1, 0, 0, True)
         regroup_weights(1, 1, 0, True)
         regroup_weights(1, 0, 1, False)
         quantise_weights(1, 0, 0)
         quantise_weights(1, 1, 0)
         read_out(0, 0, 0)
+        kv_bank = transpose_kv(1)
+        for part in range(2):
+            copy_kv(1, kv_bank, part)
         regroup_weights(1, 1, 1, False)
         project(1, 0)
         quantise_weights(1, 0, 1)

@@ -131,6 +131,25 @@ def tile_mhla2_pb_kernel(tc, q_soft, kv, W_O, grad_out, out):
             else:
                 nc.scalar.copy(out=dst, in_=src)
 
+        def chunk_columns(half, q):
+            first = HALF_COLS * half + DH * q
+            return slice(first, first + DH)
+
+        def regroup_chunk(half, g, q, on_vector):
+            dst = w_grouped[:, g, chunk_columns(half, q), :].rearrange("p (c i) t -> p c t i", i=4)
+            src = w_raw[half][g][:, :, DH * q : DH * (q + 1)].rearrange("p t (c i) -> p c t i", i=4)
+            if on_vector:
+                nc.vector.tensor_copy(out=dst, in_=src)
+            else:
+                nc.scalar.copy(out=dst, in_=src)
+
+        def quantise_chunk(half, g, q):
+            nc.vector.quantize_mx(
+                out=w_codes[:, g, chunk_columns(half, q)].bitcast(E4M3_X4),
+                scales=w_scales[:, g, chunk_columns(half, q)],
+                in_=w_grouped[:, g, chunk_columns(half, q), :].rearrange("p i t -> p (i t)"),
+            )
+
         def quantise_weights(half, g, cc):
             nc.vector.quantize_mx(
                 out=w_codes[:, g, quarter(half, cc)].bitcast(E4M3_X4),
@@ -230,12 +249,12 @@ def tile_mhla2_pb_kernel(tc, q_soft, kv, W_O, grad_out, out):
             keep_clock_up(1)
             quantise_tokens(0, tb)
         kv_bank = transpose_kv(0)
-        copy_kv(0, kv_bank, 0)
-        regroup_weights(0, 1, 0, True)
-        regroup_weights(0, 1, 1, False)
-        copy_kv(0, kv_bank, 1)
-        for cc in range(2):
-            quantise_weights(0, 1, cc)
+        for q in range(HALF_CHUNKS):
+            regroup_chunk(0, 1, q, q < 2)
+        for q in range(HALF_CHUNKS):
+            quantise_chunk(0, 1, q)
+        for part in range(2):
+            copy_kv(0, kv_bank, part)
         gy_banks = open_gy_banks()
         project_pass(0, 0, 0, gy_banks)
         for tb in range(2):
@@ -261,8 +280,8 @@ def tile_mhla2_pb_kernel(tc, q_soft, kv, W_O, grad_out, out):
         quantise_weights(1, 1, 1)
         read_out(0, 0, 4)
         read_out(1, 0, 0)
-        project(0, 1)
         read_out(1, 0, 4)
+        project(0, 1)
         project(1, 1)
         read_out(0, 1, 0)
         read_out(0, 1, 4)

@@ -50,6 +50,12 @@ def tile_mhla2_pb_kernel(tc, q_soft, kv, W_O, grad_out, out):
             for k in range(count):
                 nc.tensor.matmul(out=idle_bank[:], lhsT=zeros[:, 0:P], rhs=zeros[:], start=True, stop=True)
 
+        def keep_clock_up_behind_first_weights(count):
+            for k in range(count):
+                nc.tensor.matmul(
+                    out=idle_bank[:], lhsT=w_raw[0][0][:, PACK - 1, 0:P], rhs=w_raw[0][0][:, PACK - 1, :], start=True, stop=True
+                )
+
         tokens_raw = [
             [keep.tile([P, D], BF16, name="tokens_raw_%d_%d" % (b, tb)) for tb in range(TOKEN_BLOCKS)]
             for b in range(B)
@@ -243,10 +249,12 @@ def tile_mhla2_pb_kernel(tc, q_soft, kv, W_O, grad_out, out):
             regroup_weights(0, 0, cc, True)
         for cc in range(2):
             quantise_weights(0, 0, cc)
-        keep_clock_up(4)
+        keep_clock_up(3)
+        keep_clock_up_behind_first_weights(2)
         for tb in range(TOKEN_BLOCKS):
             transpose_tokens(0, tb)
-            keep_clock_up(1)
+            if tb > 0:
+                keep_clock_up(1)
             quantise_tokens(0, tb)
         kv_bank = transpose_kv(0)
         for q in range(HALF_CHUNKS):

from contextlib import ExitStack

import concourse.masks as masks
import concourse.mybir as mybir

F32 = mybir.dt.float32
BF16 = mybir.dt.bfloat16
U32 = mybir.dt.uint32
U8 = mybir.dt.uint8
E4M3_X4 = mybir.dt.float8_e4m3fn_x4
E5M2_X4 = mybir.dt.float8_e5m2_x4

P = 128
B, S, D, H = 2, 512, 1024, 8
DH = D // H
PACK = 4
K_PASS = P * PACK
PASSES = D // K_PASS
TOKEN_BLOCKS = S // P
HEAD_ROWS = S // H
HALVES = 2
HALF_COLS = D // HALVES
HALF_CHUNKS = HALF_COLS // DH
QUARTER_COLS = HALF_COLS // 2

FLOPS = 2 * B * S * D * D + 2 * B * H * S * DH * DH
BYTES = 2 * (B * H * DH * DH + D * D + B * S * D) + 4 * B * H * S * DH


def tile_mhla2_pb_kernel(tc, q_soft, kv, W_O, grad_out, out):
    nc = tc.nc
    with ExitStack() as ctx:
        keep = ctx.enter_context(tc.tile_pool(name="keep", bufs=1))
        stage = ctx.enter_context(tc.tile_pool(name="stage", bufs=8))
        banks = ctx.enter_context(tc.psum_pool(name="banks", bufs=8))
        ctx.enter_context(tc.manual_schedule())

        ident_f32 = keep.tile([P, P], F32)
        masks.make_identity(nc, ident_f32[:])
        ident_bf16 = keep.tile([P, P], BF16)
        masks.make_identity(nc, ident_bf16[:])
        table_warmer = keep.tile([P, 1], BF16)
        nc.scalar.copy(out=table_warmer[:], in_=ident_bf16[:, 0:1])

        zeros = keep.tile([P, S], BF16)
        nc.vector.memset(zeros[:], 0.0)
        idle_bank = banks.tile([P, S], F32, tag="bank")

        def keep_clock_up(count):
            for k in range(count):
                nc.tensor.matmul(out=idle_bank[:], lhsT=zeros[:, 0:P], rhs=zeros[:], start=True, stop=True)

        def keep_clock_up_behind_first_weights(count):
            for k in range(count):
                nc.tensor.matmul(
                    out=idle_bank[:], lhsT=w_raw[0][0][:, PACK - 1, 0:P], rhs=w_raw[0][0][:, PACK - 1, :], start=True, stop=True
                )

        tokens_raw = [
            [keep.tile([P, D], BF16, name="tokens_raw_%d_%d" % (b, tb)) for tb in range(TOKEN_BLOCKS)]
            for b in range(B)
        ]
        tokens_grouped = [
            [
                keep.tile([P, PASSES, P * PACK], BF16, name="tokens_grouped_%d_%d" % (b, tb), align_bytes=64)
                for tb in range(TOKEN_BLOCKS)
            ]
            for b in range(B)
        ]
        tokens_codes = [keep.tile([P, PASSES, S], U32, name="tokens_codes_%d" % b, align_bytes=64) for b in range(B)]
        tokens_scales = [keep.tile([P, PASSES, S], U8, name="tokens_scales_%d" % b, align_bytes=64) for b in range(B)]
        w_raw = [
            [keep.tile([P, PACK, HALF_COLS], BF16, name="w_raw_%d_%d" % (half, g)) for g in range(PASSES)]
            for half in range(HALVES)
        ]
        w_grouped = keep.tile([P, PASSES, D, PACK], BF16, align_bytes=64)
        w_codes = keep.tile([P, PASSES, D], U32, align_bytes=64)
        w_scales = keep.tile([P, PASSES, D], U8, align_bytes=64)
        kv_raw = [keep.tile([P, H, DH], BF16, name="kv_raw_%d" % b) for b in range(B)]
        kv_t = [keep.tile([P, H, DH], F32, name="kv_t_%d" % b) for b in range(B)]
        gy_t = [
            [[keep.tile([P, H, P], F32, name="gy_t_%d_%d_%d" % (b, half, j)) for j in range(2)] for half in range(HALVES)]
            for b in range(B)
        ]

        def copy_out_of_psum(index, dst, src):
            if index % 2 == 0:
                nc.vector.tensor_copy(out=dst, in_=src)
            else:
                nc.scalar.copy(out=dst, in_=src)

        def load_tokens(b):
            for tb in range(TOKEN_BLOCKS):
                nc.sync.dma_start(out=tokens_raw[b][tb][:], in_=grad_out[b, P * tb : P * (tb + 1), :])

        def load_weights(half, g):
            cols = slice(HALF_COLS * half, HALF_COLS * (half + 1))
            for u in range(2):
                first = K_PASS * g + 2 * P * u
                nc.sync.dma_start(
                    out=w_raw[half][g][:, 2 * u : 2 * u + 2, :],
                    in_=W_O[first : first + 2 * P, cols].rearrange("(p e) i -> p e i", e=2),
                )

        def load_kv(b):
            nc.sync.dma_start(out=kv_raw[b][:], in_=kv[b].rearrange("h d e -> (h d) e").rearrange("(p k) e -> p k e", k=H))

        def transpose_tokens(b, tb):
            grouped_words = tokens_grouped[b][tb][:].rearrange("p g x -> p (g x)").bitcast(F32)
            grouped_words = grouped_words.rearrange("p (g r u) -> p g r u", g=PASSES, u=2)
            words = tokens_raw[b][tb][:].bitcast(F32)
            words_t = banks.tile([P, PASSES, 2, P], F32, tag="bank")
            for g in range(PASSES):
                for u in range(2):
                    first = (2 * g + u) * P
                    nc.tensor.transpose(words_t[:, g, u, :], words[:, first : first + P], ident_f32[:])
            nc.scalar.copy(out=grouped_words, in_=words_t[:].rearrange("p g u r -> p g r u"))

        def quantise_tokens(b, tb):
            block = slice(P * tb, P * (tb + 1))
            for g in range(PASSES):
                nc.vector.quantize_mx(
                    out=tokens_codes[b][:, g, block].bitcast(E5M2_X4),
                    scales=tokens_scales[b][:, g, block],
                    in_=tokens_grouped[b][tb][:, g, :],
                )

        def quarter(half, cc):
            first = HALF_COLS * half + QUARTER_COLS * cc
            return slice(first, first + QUARTER_COLS)

        def regroup_weights(half, g, cc, on_vector):
            dst = w_grouped[:, g, quarter(half, cc), :].rearrange("p (c i) t -> p c t i", i=4)
            src = w_raw[half][g][:, :, QUARTER_COLS * cc : QUARTER_COLS * (cc + 1)].rearrange("p t (c i) -> p c t i", i=4)
            if on_vector:
                nc.vector.tensor_copy(out=dst, in_=src)
            else:
                nc.scalar.copy(out=dst, in_=src)

        def chunk_columns(half, q):
            first = HALF_COLS * half + DH * q
            return slice(first, first + DH)

        def regroup_chunk(half, g, q, on_vector):
            dst = w_grouped[:, g, chunk_columns(half, q), :].rearrange("p (c i) t -> p c t i", i=4)
            src = w_raw[half][g][:, :, DH * q : DH * (q + 1)].rearrange("p t (c i) -> p c t i", i=4)
            if on_vector:
                nc.vector.tensor_copy(out=dst, in_=src)
            else:
                nc.scalar.copy(out=dst, in_=src)

        def quantise_chunk(half, g, q):
            nc.vector.quantize_mx(
                out=w_codes[:, g, chunk_columns(half, q)].bitcast(E4M3_X4),
                scales=w_scales[:, g, chunk_columns(half, q)],
                in_=w_grouped[:, g, chunk_columns(half, q), :].rearrange("p i t -> p (i t)"),
            )

        def quantise_weights(half, g, cc):
            nc.vector.quantize_mx(
                out=w_codes[:, g, quarter(half, cc)].bitcast(E4M3_X4),
                scales=w_scales[:, g, quarter(half, cc)],
                in_=w_grouped[:, g, quarter(half, cc), :].rearrange("p i t -> p (i t)"),
            )

        def transpose_kv(b):
            kv_bank = banks.tile([P, H, DH], BF16, tag="bank")
            for k in range(H):
                nc.tensor.transpose(kv_bank[:, k, :], kv_raw[b][:, k, :], ident_bf16[:])
            return kv_bank

        def copy_kv(b, kv_bank, part):
            heads = slice(H // 2 * part, H // 2 * (part + 1))
            nc.scalar.copy(
                out=kv_t[b][:, heads, :].rearrange("p h (x k) -> p (h x) k", k=H),
                in_=kv_bank[:, :, P // 2 * part : P // 2 * (part + 1)].rearrange("p k m -> p m k"),
            )

        def open_gy_banks():
            return [banks.tile([P, S], F32, tag="bank", name="gy_bank_%d" % q) for q in range(HALF_CHUNKS)]

        def project_pass(b, half, g, gy_banks):
            for q in range(HALF_CHUNKS):
                first = HALF_COLS * half + DH * q
                nc.tensor.matmul_mx(
                    out=gy_banks[q][:],
                    lhsT=w_codes[:, g, first : first + DH].bitcast(E4M3_X4),
                    lhsT_scale=w_scales[:, g, first : first + DH],
                    rhs=tokens_codes[b][:, g, :].bitcast(E5M2_X4),
                    rhs_scale=tokens_scales[b][:, g, :],
                    start=(g == 0),
                    stop=(g == PASSES - 1),
                )

        def copy_gy(b, half, gy_banks):
            for q in range(HALF_CHUNKS):
                cc, j = divmod(q, 2)
                copy_out_of_psum(
                    q,
                    gy_t[b][half][j][:, :, HEAD_ROWS * cc : HEAD_ROWS * (cc + 1)],
                    gy_banks[q][:].rearrange("p (h r) -> p h r", h=H),
                )

        def project(b, half):
            gy_banks = open_gy_banks()
            for g in range(PASSES):
                project_pass(b, half, g, gy_banks)
            copy_gy(b, half, gy_banks)

        def read_out_matmul(b, half, head, j, dst):
            nc.tensor.matmul(
                out=dst, lhsT=gy_t[b][half][j][:, head, :], rhs=kv_t[b][:, head, :], start=True, stop=True
            )

        def store(index, b, half, first_head, heads, out_bank):
            out_rows = stage.tile([P, heads, 2 * DH], F32, tag="out_rows")
            copy_out_of_psum(index, out_rows[:], out_bank[:].rearrange("p i j d -> p i (j d)"))
            dst = out[b, first_head : first_head + heads].rearrange(
                "i (r a cc j) d -> a cc r i (j d)", a=HALVES, cc=2, j=2
            )
            for cc in range(2):
                nc.sync.dma_start(out=dst[half, cc], in_=out_rows[HEAD_ROWS * cc : HEAD_ROWS * (cc + 1), :, :])

        def read_out(b, half, first_head):
            out_banks = [banks.tile([P, 2, 2, DH], F32, tag="bank", name="out_bank_%d" % k) for k in range(2)]
            for j in range(2):
                for i in range(4):
                    read_out_matmul(b, half, first_head + i, j, out_banks[i // 2][:, i % 2, j, :])
            for k in range(2):
                store(k, b, half, first_head + 2 * k, 2, out_banks[k])

        def read_out_last(b, half, first_head):
            for i in range(4):
                out_bank = banks.tile([P, 1, 2, DH], F32, tag="bank")
                for j in range(2):
                    read_out_matmul(b, half, first_head + i, j, out_bank[:, 0, j, :])
                store(i + 1, b, half, first_head + i, 1, out_bank)

        load_weights(0, 0)
        load_tokens(0)
        load_kv(0)
        load_weights(0, 1)
        load_tokens(1)
        load_kv(1)
        load_weights(1, 0)
        load_weights(1, 1)

        for cc in range(2):
            regroup_weights(0, 0, cc, True)
        for cc in range(2):
            quantise_weights(0, 0, cc)
        keep_clock_up(3)
        keep_clock_up_behind_first_weights(2)
        for tb in range(TOKEN_BLOCKS):
            transpose_tokens(0, tb)
            if tb > 0:
                keep_clock_up(1)
            quantise_tokens(0, tb)
        kv_bank = transpose_kv(0)
        for q in range(HALF_CHUNKS):
            regroup_chunk(0, 1, q, q < 2)
        for q in range(HALF_CHUNKS):
            quantise_chunk(0, 1, q)
        for part in range(2):
            copy_kv(0, kv_bank, part)
        gy_banks = open_gy_banks()
        project_pass(0, 0, 0, gy_banks)
        for tb in range(2):
            transpose_tokens(1, tb)
        project_pass(0, 0, 1, gy_banks)
        copy_gy(0, 0, gy_banks)
        for tb in range(2, TOKEN_BLOCKS):
            transpose_tokens(1, tb)
        for tb in range(TOKEN_BLOCKS):
            quantise_tokens(1, tb)
        regroup_weights(1, 0, 0, True)
        regroup_weights(1, 1, 0, True)
        regroup_weights(1, 0, 1, False)
        quantise_weights(1, 0, 0)
        quantise_weights(1, 1, 0)
        read_out(0, 0, 0)
        kv_bank = transpose_kv(1)
        for part in range(2):
            copy_kv(1, kv_bank, part)
        regroup_weights(1, 1, 1, False)
        project(1, 0)
        quantise_weights(1, 0, 1)
        quantise_weights(1, 1, 1)
        read_out(0, 0, 4)
        read_out(1, 0, 0)
        read_out(1, 0, 4)
        project(0, 1)
        project(1, 1)
        read_out(0, 1, 0)
        read_out(0, 1, 4)
        read_out(1, 1, 0)
        read_out_last(1, 1, 4)
